import numpy as np
import ml_dtypes


def mxq(x, axis, fmt="e4m3"):
    dtype, down = {"e4m3": (ml_dtypes.float8_e4m3fn, 7), "e5m2": (ml_dtypes.float8_e5m2, 14)}[fmt]
    v = np.moveaxis(np.asarray(x, np.float32).astype(ml_dtypes.bfloat16).astype(np.float64), axis, -1)
    blocks = v.reshape(v.shape[:-1] + (-1, 32))
    amax = np.abs(blocks).max(-1, keepdims=True)
    byte = np.maximum(np.where(amax > 0, np.frexp(amax)[1] - 1 + 127, 0) - down, 1)
    scale = np.exp2(byte - 127.0)
    codes = (blocks / scale).astype(np.float32).astype(dtype).astype(np.float64)
    return np.moveaxis((codes * scale).reshape(v.shape), -1, axis)


WIDE = False


def mx_kscale(k):
    if not WIDE:
        return np.ones(k)
    levels = np.array([10, -10, 5, -5, 0])
    if k % 512:
        return np.exp2(np.random.permutation(np.resize(levels, k // 32))).repeat(32)
    a = np.empty((k // 512, 16))
    for p in range(k // 512):
        a[p, :8] = np.random.permutation(np.resize(levels, 8))
        for g in range(8):
            far = levels[np.abs(levels - a[p, g]) >= 10]
            a[p, g + 8] = far[np.random.randint(len(far))]
    return np.exp2(a.ravel()).repeat(32)


BF16 = ml_dtypes.bfloat16


def bf(x):
    return np.asarray(x, np.float32).astype(BF16)


def f64(x):
    return np.asarray(x).astype(np.float64)


B, S, H, I = 2, 2048, 512, 512


def silu(v):
    return v / (1.0 + np.exp(-v))


def ternary(shape):
    return np.random.randint(-1, 2, shape).astype(np.float64)


def draw0():
    s, t = mx_kscale(H), mx_kscale(I)
    x = np.random.standard_normal((B, S, H)) * s
    gate_w = ternary((I, H)) / s[None, :]
    up_w = ternary((I, H)) / s[None, :]
    down_w = ternary((H, I)) / t[None, :]
    gate_s = np.random.uniform(0.5, 2.5, I) / np.sqrt(H)
    up_s = np.random.uniform(0.5, 2.5, I) / np.sqrt(H) * t
    down_s = np.random.uniform(0.5, 2.5, H) / np.sqrt(I)
    return {"x": bf(x), "gate_w": bf(gate_w), "up_w": bf(up_w), "down_w": bf(down_w),
            "gate_s": bf(gate_s), "up_s": bf(up_s), "down_s": bf(down_s)}


def core(x, gate_w, up_w, down_w, gate_s, up_s, down_s):
    x = f64(x)
    b, s, h = x.shape
    xq = mxq(x.reshape(b * s, h), 1, "e4m3")
    g = (xq @ mxq(f64(gate_w), 1, "e4m3").T) * f64(gate_s)
    u = (xq @ mxq(f64(up_w), 1, "e4m3").T) * f64(up_s)
    hdn = silu(g) * u
    out = (mxq(hdn, 1, "e4m3") @ mxq(f64(down_w), 1, "e4m3").T) * f64(down_s)
    return out.reshape(b, s, -1)


def e4m3fn_bytes(y):
    return np.clip(np.asarray(y, np.float64), -448.0, 448.0).astype(np.float32).astype(ml_dtypes.float8_e4m3fn).view(np.uint8)


def e4m3fn_values(b):
    return np.asarray(b, np.uint8).view(ml_dtypes.float8_e4m3fn).astype(np.float64)


def setup_inputs():
    d = draw0()
    x0 = np.asarray(d['x']).astype(np.float64)
    s = (np.max(np.abs(x0), axis=(0, 1), keepdims=True) / 448.0).astype(np.float32)
    out = {}
    for k, v in d.items():
        if k == 'x':
            out['x_bytes'] = e4m3fn_bytes(x0 / s.astype(np.float64))
            out['x_scale'] = s
        else:
            out[k] = v
    return out


def reference(x_bytes, x_scale, gate_w, up_w, down_w, gate_s, up_s, down_s):
    return core(e4m3fn_values(x_bytes) * x_scale.astype(np.float64), gate_w, up_w, down_w, gate_s, up_s, down_s)

@@ -1,0 +1,250 @@
+from contextlib import ExitStack
+
+import concourse.mybir as mybir
+from concourse.masks import make_identity
+
+TOKENS, H, I = 4096, 512, 512
+FLOPS = 3 * 2 * TOKENS * H * I
+
+F32 = mybir.dt.float32
+BF16 = mybir.dt.bfloat16
+U32 = mybir.dt.uint32
+U8 = mybir.dt.uint8
+FP8 = mybir.dt.float8_e4m3fn
+FP8X4 = mybir.dt.float8_e4m3fn_x4
+MULT = mybir.AluOpType.mult
+SILU = mybir.ActivationFunctionType.Silu
+
+P = 128
+SUB = 4
+GROUP = P * SUB
+N_GROUPS = TOKENS // GROUP
+
+
+def tile_cudaternaryexpertmodule_t_kernel(
+    tc, x_bytes, x_scale, gate_w, up_w, down_w, gate_s, up_s, down_s, out
+):
+    nc = tc.nc
+    x_view = x_bytes.rearrange("b s k -> (b s) k").rearrange("(g p j) k -> g p j k", p=P, j=SUB)
+    out_view = out.rearrange("b s k -> (b s) k").rearrange("(g p j) k -> g p j k", p=P, j=SUB)
+
+    with ExitStack() as ctx:
+        keep = ctx.enter_context(tc.tile_pool(name="keep", bufs=1))
+        xin = ctx.enter_context(tc.tile_pool(name="xin", bufs=N_GROUPS))
+        win = ctx.enter_context(tc.tile_pool(name="win", bufs=3))
+        work = ctx.enter_context(tc.tile_pool(name="work", bufs=2))
+        outp = ctx.enter_context(tc.tile_pool(name="outp", bufs=3))
+        ps_t = ctx.enter_context(tc.psum_pool(name="ps_t", bufs=2))
+        ps_g = ctx.enter_context(tc.psum_pool(name="ps_g", bufs=2))
+        ps_m = ctx.enter_context(tc.psum_pool(name="ps_m", bufs=4))
+
+        ident = keep.tile([P, P], F32, name="ident")
+        make_identity(nc, ident[:])
+
+        scale_rep = keep.tile([P, 2, H], F32, name="scale_rep")
+        nc.scalar.dma_start(out=scale_rep[:, 0, :], in_=x_scale.rearrange("a b k -> (a b k)").partition_broadcast(P))
+        gs_raw = keep.tile([P, SUB], BF16, name="gs_raw")
+        us_raw = keep.tile([P, SUB], BF16, name="us_raw")
+        nc.scalar.dma_start(out=gs_raw[:], in_=gate_s.rearrange("(p t) -> p t", t=SUB))
+        nc.scalar.dma_start(out=us_raw[:], in_=up_s.rearrange("(p t) -> p t", t=SUB))
+        ds_rep = keep.tile([P, H], BF16, name="ds_rep")
+        nc.scalar.dma_start(out=ds_rep[:], in_=down_s.partition_broadcast(P))
+
+        x_tiles = [xin.tile([P, SUB, H], U8, name="x8") for i in range(N_GROUPS)]
+        gate_raw = win.tile([P, SUB, H], BF16, name="w_raw")
+        up_raw = win.tile([P, SUB, H], BF16, name="w_raw")
+        down_raw = win.tile([P, SUB, H], BF16, name="w_raw")
+
+        def load_w(raw, view):
+            for h in (0, 2):
+                nc.sync.dma_start(out=raw[:, h : h + 2, :], in_=view[:, h : h + 2, :])
+
+        def load_x(i):
+            nc.sync.dma_start(out=x_tiles[i][:], in_=x_view[i])
+
+        load_x(0)
+        load_w(gate_raw, gate_w.rearrange("(m t) k -> m t k", t=SUB))
+        load_w(up_raw, up_w.rearrange("(m t) k -> m t k", t=SUB))
+        load_x(1)
+        load_w(down_raw, down_w.rearrange("(r p) k -> p r k", p=P))
+        for i in range(2, N_GROUPS):
+            load_x(i)
+
+        def turn_half(raw, h, grouped):
+            words = raw.bitcast(F32)
+            bank = ps_t.tile([P, 2, 2, P], F32, name="bank_t")
+            for jj in range(2):
+                for u in range(2):
+                    w0 = (2 * h + jj) * (H // 2)
+                    nc.tensor.transpose(bank[:, jj, u, :], words[:, w0 + u : w0 + H // 2 : 2], ident[:])
+            half = grouped.bitcast(F32)[:, h * 512 : (h + 1) * 512]
+            nc.scalar.copy(
+                out=half.rearrange("p (j n u) -> p j n u", j=2, u=2),
+                in_=bank[:].rearrange("p j u n -> p j n u"),
+            )
+
+        def quantize(codes, scales, grouped):
+            nc.vector.quantize_mx(out=codes.bitcast(FP8X4), scales=scales, in_=grouped)
+
+        def turn_weight(raw):
+            grouped = work.tile([P, 4 * 512], BF16, name="w_grouped", align_bytes=64)
+            flat = raw[:].rearrange("p j k -> p (j k)")
+            for h in range(2):
+                turn_half(flat, h, grouped[:])
+            return grouped
+
+        def quantize_weight(grouped, name):
+            codes = keep.tile([P, 512], U32, name=name + "_codes", align_bytes=64)
+            scales = keep.tile([P, 512], U8, name=name + "_scales", align_bytes=64)
+            quantize(codes[:], scales[:], grouped[:])
+            return codes, scales
+
+        def widen_half(i, h, xs):
+            nc.vector.tensor_tensor(
+                out=xs[:, h * 1024 : (h + 1) * 1024],
+                in0=x_tiles[i][:, 2 * h : 2 * h + 2, :].rearrange("p j k -> p (j k)").bitcast(FP8),
+                in1=scale_rep[:].rearrange("p r k -> p (r k)"),
+                op=MULT,
+            )
+
+        def mx(dst, lhs, lc, rhs):
+            nc.tensor.matmul_mx(
+                out=dst,
+                lhsT=lhs[0][:, lc].bitcast(FP8X4),
+                lhsT_scale=lhs[1][:, lc],
+                rhs=rhs[0][:].bitcast(FP8X4),
+                rhs_scale=rhs[1][:],
+                start=True,
+                stop=True,
+            )
+
+        def cols(t):
+            return slice(P * t, P * (t + 1))
+
+        xs_t, xg_t, xq_t, sg_t, h_t, hg_t, hq_t = {}, {}, {}, {}, {}, {}, {}
+        g_ps, u_ps, d_ps = {}, {}, {}
+
+        def new_xs(i):
+            xs_t[i] = work.tile([P, SUB * H], BF16, name="xs", align_bytes=64)
+
+        def turn_x(i):
+            xg_t[i] = work.tile([P, SUB * H], BF16, name="xg", align_bytes=64)
+            for h in range(2):
+                turn_half(xs_t[i][:], h, xg_t[i][:])
+
+        def quantize_x(i):
+            c = work.tile([P, 512], U32, name="xc", align_bytes=64)
+            s = work.tile([P, 512], U8, name="xsc", align_bytes=64)
+            quantize(c[:], s[:], xg_t[i][:])
+            xq_t[i] = (c, s)
+
+        def gate_mm(i, t):
+            g_ps[t] = ps_g.tile([P, 512], F32, name="g_ps")
+            mx(g_ps[t][:], gate_q, cols(t), xq_t[i])
+
+        def up_mm(i, t):
+            u_ps[t] = ps_m.tile([P, 512], F32, name="m_ps")
+            mx(u_ps[t][:], up_q, cols(t), xq_t[i])
+
+        def silu(i, t):
+            if t == 0:
+                sg_t[i] = work.tile([P, SUB, 512], F32, name="sg")
+            nc.scalar.activation(out=sg_t[i][:, t, :], in_=g_ps[t][:], func=SILU, scale=gs[:, t : t + 1])
+
+        def stage1_front(i):
+            gate_mm(i, 0)
+            gate_mm(i, 1)
+            for t in range(SUB):
+                up_mm(i, t)
+            silu(i, 0)
+            gate_mm(i, 2)
+            silu(i, 1)
+            gate_mm(i, 3)
+            silu(i, 2)
+            silu(i, 3)
+
+        def hidden(i, t):
+            if t == 0:
+                h_t[i] = work.tile([P, SUB, 512], BF16, name="hid")
+            nc.vector.scalar_tensor_tensor(
+                out=h_t[i][:, t, :], in0=u_ps[t][:], scalar=us[:, t : t + 1], in1=sg_t[i][:, t, :], op0=MULT, op1=MULT
+            )
+
+        def interleave_half(i, h):
+            if h == 0:
+                hg_t[i] = work.tile([P, 512, 4], BF16, name="hg", align_bytes=64)
+            c = slice(256 * h, 256 * (h + 1))
+            nc.scalar.copy(out=hg_t[i][:, c, :], in_=h_t[i][:, :, c].rearrange("p t c -> p c t"))
+
+        def quantize_h(i, h):
+            if h == 0:
+                hq_t[i] = (
+                    work.tile([P, 512], U32, name="hc", align_bytes=64),
+                    work.tile([P, 512], U8, name="hsc", align_bytes=64),
+                )
+            c = slice(256 * h, 256 * (h + 1))
+            quantize(hq_t[i][0][:, c], hq_t[i][1][:, c], hg_t[i][:, c, :].rearrange("p c t -> p (c t)"))
+
+        def down_mm(i, j):
+            d_ps[j] = ps_m.tile([P, 512], F32, name="m_ps")
+            mx(d_ps[j][:], hq_t[i], cols(j), down_q)
+
+        o_t = {}
+
+        def finish(i, j):
+            if j == 0:
+                o_t[i] = outp.tile([P, SUB, 512], F32, name="o")
+            nc.vector.tensor_tensor(out=o_t[i][:, j, :], in0=d_ps[j][:], in1=ds_rep[:], op=MULT)
+            if j % 2 == 1:
+                nc.sync.dma_start(out=out_view[i][:, j - 1 : j + 1, :], in_=o_t[i][:, j - 1 : j + 1, :])
+
+        nc.vector.tensor_copy(out=scale_rep[:, 1, :], in_=scale_rep[:, 0, :])
+        gs = keep.tile([P, SUB], F32, name="gs")
+        us = keep.tile([P, SUB], F32, name="us")
+        new_xs(0)
+        new_xs(1)
+        widen_half(0, 0, xs_t[0][:])
+        gate_grouped = turn_weight(gate_raw)
+        widen_half(0, 1, xs_t[0][:])
+        gate_q = quantize_weight(gate_grouped, "gate")
+        turn_x(0)
+        up_grouped = turn_weight(up_raw)
+        widen_half(1, 0, xs_t[1][:])
+        quantize_x(0)
+        nc.vector.tensor_copy(out=gs[:], in_=gs_raw[:])
+        nc.vector.tensor_copy(out=us[:], in_=us_raw[:])
+        up_q = quantize_weight(up_grouped, "up")
+        widen_half(1, 1, xs_t[1][:])
+        stage1_front(0)
+        turn_x(1)
+        down_grouped = turn_weight(down_raw)
+        down_q = quantize_weight(down_grouped, "down")
+
+        for i in range(N_GROUPS + 1):
+            last = i == N_GROUPS
+            for j in range(SUB):
+                if not last:
+                    hidden(i, j)
+                if i > 0:
+                    down_mm(i - 1, j)
+            if not last:
+                interleave_half(i, 0)
+                interleave_half(i, 1)
+            if i > 0:
+                for j in range(SUB):
+                    finish(i - 1, j)
+            if last:
+                break
+            quantize_h(i, 0)
+            if i + 1 < N_GROUPS:
+                quantize_x(i + 1)
+            if i + 2 < N_GROUPS:
+                new_xs(i + 2)
+                widen_half(i + 2, 0, xs_t[i + 2][:])
+            quantize_h(i, 1)
+            if i + 2 < N_GROUPS:
+                widen_half(i + 2, 1, xs_t[i + 2][:])
+            if i + 1 < N_GROUPS:
+                stage1_front(i + 1)
+            if i + 2 < N_GROUPS:
+                turn_x(i + 2)

@@ -37,18 +37,28 @@ def tile_cudaternaryexpertmodule_t_kernel(
         ps_t = ctx.enter_context(tc.psum_pool(name="ps_t", bufs=2))
         ps_g = ctx.enter_context(tc.psum_pool(name="ps_g", bufs=2))
         ps_m = ctx.enter_context(tc.psum_pool(name="ps_m", bufs=4))
+        ctx.enter_context(tc.manual_schedule())
 
         ident = keep.tile([P, P], F32, name="ident")
         make_identity(nc, ident[:])
 
-        scale_rep = keep.tile([P, 2, H], F32, name="scale_rep")
-        nc.scalar.dma_start(out=scale_rep[:, 0, :], in_=x_scale.rearrange("a b k -> (a b k)").partition_broadcast(P))
+        xsc_col = keep.tile([P, SUB], F32, name="xsc_col")
         gs_raw = keep.tile([P, SUB], BF16, name="gs_raw")
         us_raw = keep.tile([P, SUB], BF16, name="us_raw")
+        ds_raw = keep.tile([P, SUB], BF16, name="ds_raw")
+        nc.scalar.dma_start(out=xsc_col[:], in_=x_scale.rearrange("a b k -> (a b k)").rearrange("(p t) -> p t", t=SUB))
         nc.scalar.dma_start(out=gs_raw[:], in_=gate_s.rearrange("(p t) -> p t", t=SUB))
         nc.scalar.dma_start(out=us_raw[:], in_=up_s.rearrange("(p t) -> p t", t=SUB))
-        ds_rep = keep.tile([P, H], BF16, name="ds_rep")
-        nc.scalar.dma_start(out=ds_rep[:], in_=down_s.partition_broadcast(P))
+        nc.scalar.dma_start(out=ds_raw[:], in_=down_s.rearrange("(p t) -> p t", t=SUB))
+        scale_rep = keep.tile([P, 2, H], F32, name="scale_rep")
+        ds_rep = keep.tile([P, H], F32, name="ds_rep")
+
+        def spread(col, copies):
+            bank = ps_g.tile([P, SUB, P], F32, name="g_ps")
+            for t in range(SUB):
+                nc.tensor.transpose(bank[:, t, :], col[:, t : t + 1].to_broadcast([P, P]), ident[:])
+            for copy, dst in copies:
+                copy(out=dst.rearrange("p (n t) -> p n t", t=SUB), in_=bank[:].rearrange("p t n -> p n t"))
 
         x_tiles = [xin.tile([P, SUB, H], U8, name="x8") for i in range(N_GROUPS)]
         gate_raw = win.tile([P, SUB, H], BF16, name="w_raw")
@@ -59,10 +69,12 @@ def tile_cudaternaryexpertmodule_t_kernel(
             for h in (0, 2):
                 nc.sync.dma_start(out=raw[:, h : h + 2, :], in_=view[:, h : h + 2, :])
 
-        def load_x(i):
-            nc.sync.dma_start(out=x_tiles[i][:], in_=x_view[i])
+        def load_x(i, parts=1):
+            n = SUB // parts
+            for h in range(parts):
+                nc.sync.dma_start(out=x_tiles[i][:, h * n : (h + 1) * n, :], in_=x_view[i][:, h * n : (h + 1) * n, :])
 
-        load_x(0)
+        load_x(0, 2)
         load_w(gate_raw, gate_w.rearrange("(m t) k -> m t k", t=SUB))
         load_w(up_raw, up_w.rearrange("(m t) k -> m t k", t=SUB))
         load_x(1)
@@ -70,7 +82,7 @@ def tile_cudaternaryexpertmodule_t_kernel(
         for i in range(2, N_GROUPS):
             load_x(i)
 
-        def turn_half(raw, h, grouped):
+        def turn_half(raw, h, grouped, copy=nc.scalar.copy):
             words = raw.bitcast(F32)
             bank = ps_t.tile([P, 2, 2, P], F32, name="bank_t")
             for jj in range(2):
@@ -78,7 +90,7 @@ def tile_cudaternaryexpertmodule_t_kernel(
                     w0 = (2 * h + jj) * (H // 2)
                     nc.tensor.transpose(bank[:, jj, u, :], words[:, w0 + u : w0 + H // 2 : 2], ident[:])
             half = grouped.bitcast(F32)[:, h * 512 : (h + 1) * 512]
-            nc.scalar.copy(
+            copy(
                 out=half.rearrange("p (j n u) -> p j n u", j=2, u=2),
                 in_=bank[:].rearrange("p j u n -> p j n u"),
             )
@@ -86,11 +98,11 @@ def tile_cudaternaryexpertmodule_t_kernel(
         def quantize(codes, scales, grouped):
             nc.vector.quantize_mx(out=codes.bitcast(FP8X4), scales=scales, in_=grouped)
 
-        def turn_weight(raw):
+        def turn_weight(raw, copy=nc.scalar.copy):
             grouped = work.tile([P, 4 * 512], BF16, name="w_grouped", align_bytes=64)
             flat = raw[:].rearrange("p j k -> p (j k)")
             for h in range(2):
-                turn_half(flat, h, grouped[:])
+                turn_half(flat, h, grouped[:], copy)
             return grouped
 
         def quantize_weight(grouped, name):
@@ -151,18 +163,6 @@ def tile_cudaternaryexpertmodule_t_kernel(
                 sg_t[i] = work.tile([P, SUB, 512], F32, name="sg")
             nc.scalar.activation(out=sg_t[i][:, t, :], in_=g_ps[t][:], func=SILU, scale=gs[:, t : t + 1])
 
-        def stage1_front(i):
-            gate_mm(i, 0)
-            gate_mm(i, 1)
-            for t in range(SUB):
-                up_mm(i, t)
-            silu(i, 0)
-            gate_mm(i, 2)
-            silu(i, 1)
-            gate_mm(i, 3)
-            silu(i, 2)
-            silu(i, 3)
-
         def hidden(i, t):
             if t == 0:
                 h_t[i] = work.tile([P, SUB, 512], BF16, name="hid")
@@ -170,11 +170,11 @@ def tile_cudaternaryexpertmodule_t_kernel(
                 out=h_t[i][:, t, :], in0=u_ps[t][:], scalar=us[:, t : t + 1], in1=sg_t[i][:, t, :], op0=MULT, op1=MULT
             )
 
-        def interleave_half(i, h):
+        def interleave_half(i, h, copy=nc.scalar.copy):
             if h == 0:
                 hg_t[i] = work.tile([P, 512, 4], BF16, name="hg", align_bytes=64)
             c = slice(256 * h, 256 * (h + 1))
-            nc.scalar.copy(out=hg_t[i][:, c, :], in_=h_t[i][:, :, c].rearrange("p t c -> p c t"))
+            copy(out=hg_t[i][:, c, :], in_=h_t[i][:, :, c].rearrange("p t c -> p c t"))
 
         def quantize_h(i, h):
             if h == 0:
@@ -195,56 +195,93 @@ def tile_cudaternaryexpertmodule_t_kernel(
             if j == 0:
                 o_t[i] = outp.tile([P, SUB, 512], F32, name="o")
             nc.vector.tensor_tensor(out=o_t[i][:, j, :], in0=d_ps[j][:], in1=ds_rep[:], op=MULT)
-            if j % 2 == 1:
-                nc.sync.dma_start(out=out_view[i][:, j - 1 : j + 1, :], in_=o_t[i][:, j - 1 : j + 1, :])
+            step = 1 if i == N_GROUPS - 1 else 2
+            if j % step == step - 1:
+                js = slice(j - step + 1, j + 1)
+                nc.sync.dma_start(out=out_view[i][:, js, :], in_=o_t[i][:, js, :])
 
-        nc.vector.tensor_copy(out=scale_rep[:, 1, :], in_=scale_rep[:, 0, :])
         gs = keep.tile([P, SUB], F32, name="gs")
         us = keep.tile([P, SUB], F32, name="us")
+        ds_col = keep.tile([P, SUB], F32, name="ds_col")
         new_xs(0)
         new_xs(1)
+        spread(xsc_col, [(nc.vector.tensor_copy, scale_rep[:, 0, :]), (nc.scalar.copy, scale_rep[:, 1, :])])
         widen_half(0, 0, xs_t[0][:])
         gate_grouped = turn_weight(gate_raw)
         widen_half(0, 1, xs_t[0][:])
-        gate_q = quantize_weight(gate_grouped, "gate")
         turn_x(0)
+        gate_q = quantize_weight(gate_grouped, "gate")
         up_grouped = turn_weight(up_raw)
-        widen_half(1, 0, xs_t[1][:])
-        quantize_x(0)
         nc.vector.tensor_copy(out=gs[:], in_=gs_raw[:])
         nc.vector.tensor_copy(out=us[:], in_=us_raw[:])
+        nc.vector.tensor_copy(out=ds_col[:], in_=ds_raw[:])
+        widen_half(1, 0, xs_t[1][:])
+        quantize_x(0)
         up_q = quantize_weight(up_grouped, "up")
         widen_half(1, 1, xs_t[1][:])
-        stage1_front(0)
+        gate_mm(0, 0)
+        gate_mm(0, 1)
+        silu(0, 0)
+        silu(0, 1)
+        up_mm(0, 0)
+        gate_mm(0, 2)
+        up_mm(0, 1)
+        gate_mm(0, 3)
+        up_mm(0, 2)
+        up_mm(0, 3)
+        silu(0, 2)
+        silu(0, 3)
         turn_x(1)
-        down_grouped = turn_weight(down_raw)
-        down_q = quantize_weight(down_grouped, "down")
 
         for i in range(N_GROUPS + 1):
-            last = i == N_GROUPS
-            for j in range(SUB):
-                if not last:
+            nxt, far = i + 1, i + 2
+            if i < N_GROUPS:
+                hidden(i, 0)
+                hidden(i, 1)
+            if nxt < N_GROUPS:
+                quantize_x(nxt)
+            if i == 1:
+                down_q = quantize_weight(down_grouped, "down")
+            if i > 0:
+                down_mm(i - 1, 0)
+                down_mm(i - 1, 1)
+            if nxt < N_GROUPS:
+                gate_mm(nxt, 0)
+                gate_mm(nxt, 1)
+                silu(nxt, 0)
+                silu(nxt, 1)
+            for j in (2, 3):
+                if i < N_GROUPS:
                     hidden(i, j)
                 if i > 0:
                     down_mm(i - 1, j)
-            if not last:
+            if i == 0:
+                new_xs(far)
+                widen_half(far, 0, xs_t[far][:])
+            if i < N_GROUPS:
                 interleave_half(i, 0)
-                interleave_half(i, 1)
-            if i > 0:
-                for j in range(SUB):
+                interleave_half(i, 1, nc.vector.tensor_copy if i in (0, N_GROUPS - 2, N_GROUPS - 1) else nc.scalar.copy)
+            if nxt < N_GROUPS:
+                gate_mm(nxt, 2)
+                gate_mm(nxt, 3)
+                silu(nxt, 2)
+                silu(nxt, 3)
+            for j in range(SUB):
+                if i > 0:
                     finish(i - 1, j)
-            if last:
+                if nxt < N_GROUPS:
+                    up_mm(nxt, j)
+            if i == N_GROUPS:
                 break
+            if far < N_GROUPS:
+                if i > 0:
+                    new_xs(far)
+                    widen_half(far, 0, xs_t[far][:])
+                widen_half(far, 1, xs_t[far][:])
             quantize_h(i, 0)
-            if i + 1 < N_GROUPS:
-                quantize_x(i + 1)
-            if i + 2 < N_GROUPS:
-                new_xs(i + 2)
-                widen_half(i + 2, 0, xs_t[i + 2][:])
             quantize_h(i, 1)
-            if i + 2 < N_GROUPS:
-                widen_half(i + 2, 1, xs_t[i + 2][:])
-            if i + 1 < N_GROUPS:
-                stage1_front(i + 1)
-            if i + 2 < N_GROUPS:
-                turn_x(i + 2)
+            if far < N_GROUPS:
+                turn_x(far)
+            if i == 0:
+                down_grouped = turn_weight(down_raw)
+                spread(ds_col, [(nc.scalar.copy, ds_rep[:])])

@@ -19,6 +19,9 @@ P = 128
 SUB = 4
 GROUP = P * SUB
 N_GROUPS = TOKENS // GROUP
+POOL_J = ()
+LAG = 2
+WIDEN = (4, 4, 2, 0, 0, 0, 0, 0, 0, 0)
 
 
 def tile_cudaternaryexpertmodule_t_kernel(
@@ -38,6 +41,14 @@ def tile_cudaternaryexpertmodule_t_kernel(
         ps_g = ctx.enter_context(tc.psum_pool(name="ps_g", bufs=2))
         ps_m = ctx.enter_context(tc.psum_pool(name="ps_m", bufs=4))
         ctx.enter_context(tc.manual_schedule())
+
+        zeros = keep.tile([P, 512], BF16, name="zeros")
+        nc.vector.memset(zeros[:], 0.0)
+
+        def warm(n):
+            bank = ps_m.tile([P, 512], F32, name="m_ps")
+            for k in range(n):
+                nc.tensor.matmul(out=bank[:], lhsT=zeros[:, 0:P], rhs=zeros[:], start=True, stop=True)
 
         ident = keep.tile([P, P], F32, name="ident")
         make_identity(nc, ident[:])
@@ -65,30 +76,29 @@ def tile_cudaternaryexpertmodule_t_kernel(
         up_raw = win.tile([P, SUB, H], BF16, name="w_raw")
         down_raw = win.tile([P, SUB, H], BF16, name="w_raw")
 
-        def load_w(raw, view):
-            for h in (0, 2):
-                nc.sync.dma_start(out=raw[:, h : h + 2, :], in_=view[:, h : h + 2, :])
-
-        def load_x(i, parts=1):
+        def load(dst, src, parts):
             n = SUB // parts
             for h in range(parts):
-                nc.sync.dma_start(out=x_tiles[i][:, h * n : (h + 1) * n, :], in_=x_view[i][:, h * n : (h + 1) * n, :])
+                nc.sync.dma_start(out=dst[:, h * n : (h + 1) * n, :], in_=src[:, h * n : (h + 1) * n, :])
 
-        load_x(0, 2)
-        load_w(gate_raw, gate_w.rearrange("(m t) k -> m t k", t=SUB))
-        load_w(up_raw, up_w.rearrange("(m t) k -> m t k", t=SUB))
-        load_x(1)
-        load_w(down_raw, down_w.rearrange("(r p) k -> p r k", p=P))
+        load(x_tiles[0], x_view[0], 2)
+        load(gate_raw, gate_w.rearrange("(m t) k -> m t k", t=SUB), 2)
+        load(up_raw, up_w.rearrange("(m t) k -> m t k", t=SUB), 2)
+        load(x_tiles[1], x_view[1], 1)
+        load(down_raw, down_w.rearrange("(r p) k -> p r k", p=P), 2)
         for i in range(2, N_GROUPS):
-            load_x(i)
+            load(x_tiles[i], x_view[i], 1)
 
-        def turn_half(raw, h, grouped, copy=nc.scalar.copy):
+        def transpose_half(raw, h):
             words = raw.bitcast(F32)
             bank = ps_t.tile([P, 2, 2, P], F32, name="bank_t")
             for jj in range(2):
                 for u in range(2):
                     w0 = (2 * h + jj) * (H // 2)
                     nc.tensor.transpose(bank[:, jj, u, :], words[:, w0 + u : w0 + H // 2 : 2], ident[:])
+            return bank
+
+        def empty_half(bank, h, grouped, copy=nc.scalar.copy):
             half = grouped.bitcast(F32)[:, h * 512 : (h + 1) * 512]
             copy(
                 out=half.rearrange("p (j n u) -> p j n u", j=2, u=2),
@@ -98,11 +108,11 @@ def tile_cudaternaryexpertmodule_t_kernel(
         def quantize(codes, scales, grouped):
             nc.vector.quantize_mx(out=codes.bitcast(FP8X4), scales=scales, in_=grouped)
 
-        def turn_weight(raw, copy=nc.scalar.copy):
-            grouped = work.tile([P, 4 * 512], BF16, name="w_grouped", align_bytes=64)
+        def turn_weight(raw, copies=(nc.scalar.copy, nc.scalar.copy)):
+            grouped = work.tile([P, SUB * H], BF16, name="w_grouped", align_bytes=64)
             flat = raw[:].rearrange("p j k -> p (j k)")
             for h in range(2):
-                turn_half(flat, h, grouped[:], copy)
+                empty_half(transpose_half(flat, h), h, grouped[:], copies[h])
             return grouped
 
         def quantize_weight(grouped, name):
@@ -111,38 +121,34 @@ def tile_cudaternaryexpertmodule_t_kernel(
             quantize(codes[:], scales[:], grouped[:])
             return codes, scales
 
-        def widen_half(i, h, xs):
+        xs_t, xg_t, xq_t, sg_t, h_t, hg_t, hq_t, o_t, x_banks = {}, {}, {}, {}, {}, {}, {}, {}, {}
+        g_ps, u_ps, d_ps = {}, {}, {}
+
+        def widen(i, j0, n=1):
+            if j0 == 0:
+                xs_t[i] = work.tile([P, SUB * H], BF16, name="xs", bufs=N_GROUPS, align_bytes=64)
             nc.vector.tensor_tensor(
-                out=xs[:, h * 1024 : (h + 1) * 1024],
-                in0=x_tiles[i][:, 2 * h : 2 * h + 2, :].rearrange("p j k -> p (j k)").bitcast(FP8),
-                in1=scale_rep[:].rearrange("p r k -> p (r k)"),
+                out=xs_t[i][:, j0 * H : (j0 + n) * H],
+                in0=x_tiles[i][:, j0 : j0 + n, :].rearrange("p j k -> p (j k)").bitcast(FP8),
+                in1=scale_rep[:, 0:n, :].rearrange("p r k -> p (r k)"),
                 op=MULT,
             )
 
-        def mx(dst, lhs, lc, rhs):
-            nc.tensor.matmul_mx(
-                out=dst,
-                lhsT=lhs[0][:, lc].bitcast(FP8X4),
-                lhsT_scale=lhs[1][:, lc],
-                rhs=rhs[0][:].bitcast(FP8X4),
-                rhs_scale=rhs[1][:],
-                start=True,
-                stop=True,
-            )
+        todo = [(i, j) for i in range(N_GROUPS) for j in range(0, SUB, 2)]
 
-        def cols(t):
-            return slice(P * t, P * (t + 1))
+        def widen_next(n):
+            for k in range(n):
+                if todo:
+                    i, j = todo.pop(0)
+                    widen(i, j, 2)
 
-        xs_t, xg_t, xq_t, sg_t, h_t, hg_t, hq_t = {}, {}, {}, {}, {}, {}, {}
-        g_ps, u_ps, d_ps = {}, {}, {}
+        def turn_x(i, h):
+            x_banks[i, h] = transpose_half(xs_t[i][:], h)
 
-        def new_xs(i):
-            xs_t[i] = work.tile([P, SUB * H], BF16, name="xs", align_bytes=64)
-
-        def turn_x(i):
-            xg_t[i] = work.tile([P, SUB * H], BF16, name="xg", align_bytes=64)
-            for h in range(2):
-                turn_half(xs_t[i][:], h, xg_t[i][:])
+        def empty_x(i, h, copy=nc.scalar.copy):
+            if h == 0:
+                xg_t[i] = work.tile([P, SUB * H], BF16, name="xg", bufs=3, align_bytes=64)
+            empty_half(x_banks[i, h], h, xg_t[i][:], copy)
 
         def quantize_x(i):
             c = work.tile([P, 512], U32, name="xc", align_bytes=64)
@@ -150,13 +156,29 @@ def tile_cudaternaryexpertmodule_t_kernel(
             quantize(c[:], s[:], xg_t[i][:])
             xq_t[i] = (c, s)
 
+        def mx(dst, lhs, t, rhs):
+            c = slice(P * t, P * (t + 1))
+            nc.tensor.matmul_mx(
+                out=dst,
+                lhsT=lhs[0][:, c].bitcast(FP8X4),
+                lhsT_scale=lhs[1][:, c],
+                rhs=rhs[0][:].bitcast(FP8X4),
+                rhs_scale=rhs[1][:],
+                start=True,
+                stop=True,
+            )
+
         def gate_mm(i, t):
             g_ps[t] = ps_g.tile([P, 512], F32, name="g_ps")
-            mx(g_ps[t][:], gate_q, cols(t), xq_t[i])
+            mx(g_ps[t][:], gate_q, t, xq_t[i])
 
         def up_mm(i, t):
-            u_ps[t] = ps_m.tile([P, 512], F32, name="m_ps")
-            mx(u_ps[t][:], up_q, cols(t), xq_t[i])
+            u_ps[i, t] = ps_m.tile([P, 512], F32, name="m_ps")
+            mx(u_ps[i, t][:], up_q, t, xq_t[i])
+
+        def down_mm(i, j):
+            d_ps[i, j] = ps_m.tile([P, 512], F32, name="m_ps")
+            mx(d_ps[i, j][:], hq_t[i], j, down_q)
 
         def silu(i, t):
             if t == 0:
@@ -167,11 +189,11 @@ def tile_cudaternaryexpertmodule_t_kernel(
             if t == 0:
                 h_t[i] = work.tile([P, SUB, 512], BF16, name="hid")
             nc.vector.scalar_tensor_tensor(
-                out=h_t[i][:, t, :], in0=u_ps[t][:], scalar=us[:, t : t + 1], in1=sg_t[i][:, t, :], op0=MULT, op1=MULT
+                out=h_t[i][:, t, :], in0=u_ps[i, t][:], scalar=us[:, t : t + 1], in1=sg_t[i][:, t, :], op0=MULT, op1=MULT
             )
 
         def interleave_half(i, h, copy=nc.scalar.copy):
-            if h == 0:
+            if i not in hg_t:
                 hg_t[i] = work.tile([P, 512, 4], BF16, name="hg", align_bytes=64)
             c = slice(256 * h, 256 * (h + 1))
             copy(out=hg_t[i][:, c, :], in_=h_t[i][:, :, c].rearrange("p t c -> p c t"))
@@ -183,105 +205,144 @@ def tile_cudaternaryexpertmodule_t_kernel(
                     work.tile([P, 512], U8, name="hsc", align_bytes=64),
                 )
             c = slice(256 * h, 256 * (h + 1))
+            h_ready.add((i, h))
             quantize(hq_t[i][0][:, c], hq_t[i][1][:, c], hg_t[i][:, c, :].rearrange("p c t -> p (c t)"))
 
-        def down_mm(i, j):
-            d_ps[j] = ps_m.tile([P, 512], F32, name="m_ps")
-            mx(d_ps[j][:], hq_t[i], cols(j), down_q)
+        done = set()
 
-        o_t = {}
+        def store(i, j):
+            done.add((i, j))
+            a = j - j % 2
+            if i == N_GROUPS - 1:
+                nc.sync.dma_start(out=out_view[i][:, j, :], in_=o_t[i][:, j, :])
+            elif (i, a) in done and (i, a + 1) in done:
+                nc.sync.dma_start(out=out_view[i][:, a : a + 2, :], in_=o_t[i][:, a : a + 2, :])
 
         def finish(i, j):
-            if j == 0:
+            if i not in o_t:
                 o_t[i] = outp.tile([P, SUB, 512], F32, name="o")
-            nc.vector.tensor_tensor(out=o_t[i][:, j, :], in0=d_ps[j][:], in1=ds_rep[:], op=MULT)
-            step = 1 if i == N_GROUPS - 1 else 2
-            if j % step == step - 1:
-                js = slice(j - step + 1, j + 1)
-                nc.sync.dma_start(out=out_view[i][:, js, :], in_=o_t[i][:, js, :])
+            if j in POOL_J and i < N_GROUPS - 1:
+                raw = work.tile([P, 512], F32, name="o_raw")
+                nc.scalar.copy(out=raw[:], in_=d_ps[i, j][:])
+                nc.gpsimd.tensor_tensor(out=o_t[i][:, j, :], in0=raw[:], in1=ds_rep[:], op=MULT)
+            else:
+                nc.vector.tensor_tensor(out=o_t[i][:, j, :], in0=d_ps[i, j][:], in1=ds_rep[:], op=MULT)
+            store(i, j)
+
+        order = []
+        for i in range(N_GROUPS + LAG):
+            for t in range(SUB):
+                if i < N_GROUPS:
+                    order.append((hidden, up_mm, i, t))
+                if i >= LAG:
+                    order.append((finish, down_mm, i - LAG, t))
+        emptied, filled, h_ready = [], [], set()
+
+        def pump():
+            while len(filled) < min(len(order), len(emptied) + 4):
+                what, filler, i, t = order[len(filled)]
+                if filler == up_mm and i not in xq_t:
+                    return
+                if filler == down_mm and (i, t // 2) not in h_ready:
+                    return
+                filler(i, t)
+                filled.append(t)
+
+        def empty_next():
+            what, filler, i, t = order[len(emptied)]
+            what(i, t)
+            emptied.append(t)
+            pump()
 
         gs = keep.tile([P, SUB], F32, name="gs")
         us = keep.tile([P, SUB], F32, name="us")
         ds_col = keep.tile([P, SUB], F32, name="ds_col")
-        new_xs(0)
-        new_xs(1)
+        warm(5)
         spread(xsc_col, [(nc.vector.tensor_copy, scale_rep[:, 0, :]), (nc.scalar.copy, scale_rep[:, 1, :])])
-        widen_half(0, 0, xs_t[0][:])
+        widen_next(1)
+        warm(2)
         gate_grouped = turn_weight(gate_raw)
-        widen_half(0, 1, xs_t[0][:])
-        turn_x(0)
+        widen_next(1)
+        warm(2)
+        for h in range(2):
+            turn_x(0, h)
+            empty_x(0, h)
         gate_q = quantize_weight(gate_grouped, "gate")
+        warm(2)
         up_grouped = turn_weight(up_raw)
         nc.vector.tensor_copy(out=gs[:], in_=gs_raw[:])
         nc.vector.tensor_copy(out=us[:], in_=us_raw[:])
         nc.vector.tensor_copy(out=ds_col[:], in_=ds_raw[:])
-        widen_half(1, 0, xs_t[1][:])
+        widen_next(1)
         quantize_x(0)
-        up_q = quantize_weight(up_grouped, "up")
-        widen_half(1, 1, xs_t[1][:])
         gate_mm(0, 0)
         gate_mm(0, 1)
+        widen_next(2)
+        up_q = quantize_weight(up_grouped, "up")
         silu(0, 0)
-        silu(0, 1)
-        up_mm(0, 0)
         gate_mm(0, 2)
-        up_mm(0, 1)
+        silu(0, 1)
         gate_mm(0, 3)
-        up_mm(0, 2)
-        up_mm(0, 3)
-        silu(0, 2)
-        silu(0, 3)
-        turn_x(1)
+        pump()
+        for h in range(2):
+            turn_x(1, h)
+            empty_x(1, h)
+        widen_next(2)
 
-        for i in range(N_GROUPS + 1):
-            nxt, far = i + 1, i + 2
+        for i in range(N_GROUPS + LAG):
+            nxt, near, old = i + 1, i + 2, i - 1
+            has_old = 0 <= old < N_GROUPS
+
+            def block(b):
+                if i < N_GROUPS:
+                    empty_next()
+                if i >= LAG:
+                    empty_next()
+                widen_next((WIDEN[i] + 3 - b) // 4)
+
             if i < N_GROUPS:
-                hidden(i, 0)
-                hidden(i, 1)
+                silu(i, 2)
+            if old == N_GROUPS - 1:
+                interleave_half(old, 1, nc.vector.tensor_copy)
+            block(0)
             if nxt < N_GROUPS:
                 quantize_x(nxt)
+                gate_mm(nxt, 0)
+                pump()
+            if has_old:
+                interleave_half(old, 0)
+            if i < N_GROUPS:
+                silu(i, 3)
+            if nxt < N_GROUPS:
+                gate_mm(nxt, 1)
+            if near < N_GROUPS:
+                turn_x(near, 0)
+            if i == 0:
+                empty_x(near, 0)
+            block(1)
+            if has_old and old < N_GROUPS - 1:
+                interleave_half(old, 1)
+            if near < N_GROUPS:
+                turn_x(near, 1)
+            if i == 0:
+                empty_x(near, 1)
             if i == 1:
                 down_q = quantize_weight(down_grouped, "down")
-            if i > 0:
-                down_mm(i - 1, 0)
-                down_mm(i - 1, 1)
+            if has_old:
+                quantize_h(old, 0)
             if nxt < N_GROUPS:
-                gate_mm(nxt, 0)
-                gate_mm(nxt, 1)
                 silu(nxt, 0)
-                silu(nxt, 1)
-            for j in (2, 3):
-                if i < N_GROUPS:
-                    hidden(i, j)
-                if i > 0:
-                    down_mm(i - 1, j)
-            if i == 0:
-                new_xs(far)
-                widen_half(far, 0, xs_t[far][:])
-            if i < N_GROUPS:
-                interleave_half(i, 0)
-                interleave_half(i, 1, nc.vector.tensor_copy if i in (0, N_GROUPS - 2, N_GROUPS - 1) else nc.scalar.copy)
-            if nxt < N_GROUPS:
                 gate_mm(nxt, 2)
-                gate_mm(nxt, 3)
-                silu(nxt, 2)
-                silu(nxt, 3)
-            for j in range(SUB):
-                if i > 0:
-                    finish(i - 1, j)
-                if nxt < N_GROUPS:
-                    up_mm(nxt, j)
-            if i == N_GROUPS:
-                break
-            if far < N_GROUPS:
-                if i > 0:
-                    new_xs(far)
-                    widen_half(far, 0, xs_t[far][:])
-                widen_half(far, 1, xs_t[far][:])
-            quantize_h(i, 0)
-            quantize_h(i, 1)
-            if far < N_GROUPS:
-                turn_x(far)
+                silu(nxt, 1)
+            block(2)
             if i == 0:
                 down_grouped = turn_weight(down_raw)
                 spread(ds_col, [(nc.scalar.copy, ds_rep[:])])
+            if has_old:
+                quantize_h(old, 1)
+            if nxt < N_GROUPS:
+                gate_mm(nxt, 3)
+            if near < N_GROUPS and i > 0:
+                empty_x(near, 0)
+                empty_x(near, 1)
+            block(3)

@@ -19,9 +19,10 @@ P = 128
 SUB = 4
 GROUP = P * SUB
 N_GROUPS = TOKENS // GROUP
-POOL_J = ()
+POOL_OUT = {(i, 3) for i in range(2, 6)}
+POOL_IL = {(i, 1) for i in range(3, 7)}
 LAG = 2
-WIDEN = (4, 4, 2, 0, 0, 0, 0, 0, 0, 0)
+WIDEN = (4, 4, 3, 0, 0, 0, 0, 0, 0, 0)
 
 
 def tile_cudaternaryexpertmodule_t_kernel(
@@ -45,8 +46,8 @@ def tile_cudaternaryexpertmodule_t_kernel(
         zeros = keep.tile([P, 512], BF16, name="zeros")
         nc.vector.memset(zeros[:], 0.0)
 
-        def warm(n):
-            bank = ps_m.tile([P, 512], F32, name="m_ps")
+        def warm(n, pool=ps_m, tag="m_ps"):
+            bank = pool.tile([P, 512], F32, name=tag)
             for k in range(n):
                 nc.tensor.matmul(out=bank[:], lhsT=zeros[:, 0:P], rhs=zeros[:], start=True, stop=True)
 
@@ -192,7 +193,12 @@ def tile_cudaternaryexpertmodule_t_kernel(
                 out=h_t[i][:, t, :], in0=u_ps[i, t][:], scalar=us[:, t : t + 1], in1=sg_t[i][:, t, :], op0=MULT, op1=MULT
             )
 
+        def pool_copy(out, in_):
+            nc.gpsimd.tensor_scalar(out=out, in0=in_, scalar1=1.0, scalar2=0.0, op0=MULT, op1=mybir.AluOpType.add)
+
         def interleave_half(i, h, copy=nc.scalar.copy):
+            if (i, h) in POOL_IL:
+                copy = pool_copy
             if i not in hg_t:
                 hg_t[i] = work.tile([P, 512, 4], BF16, name="hg", align_bytes=64)
             c = slice(256 * h, 256 * (h + 1))
@@ -220,22 +226,36 @@ def tile_cudaternaryexpertmodule_t_kernel(
 
         def finish(i, j):
             if i not in o_t:
-                o_t[i] = outp.tile([P, SUB, 512], F32, name="o")
-            if j in POOL_J and i < N_GROUPS - 1:
-                raw = work.tile([P, 512], F32, name="o_raw")
-                nc.scalar.copy(out=raw[:], in_=d_ps[i, j][:])
-                nc.gpsimd.tensor_tensor(out=o_t[i][:, j, :], in0=raw[:], in1=ds_rep[:], op=MULT)
-            else:
-                nc.vector.tensor_tensor(out=o_t[i][:, j, :], in0=d_ps[i, j][:], in1=ds_rep[:], op=MULT)
+                o_t[i] = outp.tile([P, SUB, 512], F32, name="o", bufs=4)
+            nc.vector.tensor_tensor(out=o_t[i][:, j, :], in0=d_ps[i, j][:], in1=ds_rep[:], op=MULT)
+            store(i, j)
+
+        def pool_mm(i, j):
+            d_ps[i, j] = ps_g.tile([P, 512], F32, name="g_ps")
+            mx(d_ps[i, j][:], hq_t[i], j, down_q)
+
+        def finish_pool(i, j):
+            if i not in o_t:
+                o_t[i] = outp.tile([P, SUB, 512], F32, name="o", bufs=4)
+            raw = work.tile([P, 512], F32, name="o_raw")
+            nc.scalar.copy(out=raw[:], in_=d_ps[i, j][:])
+            nc.gpsimd.tensor_tensor(out=o_t[i][:, j, :], in0=raw[:], in1=ds_rep[:], op=MULT)
             store(i, j)
 
         order = []
         for i in range(N_GROUPS + LAG):
             for t in range(SUB):
+                if i >= LAG and (i - LAG, 3) in POOL_OUT:
+                    continue
                 if i < N_GROUPS:
                     order.append((hidden, up_mm, i, t))
                 if i >= LAG:
                     order.append((finish, down_mm, i - LAG, t))
+            if i >= LAG and (i - LAG, 3) in POOL_OUT:
+                for what in "hfhfhfh":
+                    n = sum(o[2] == (i if what == "h" else i - LAG) and o[0] == (hidden if what == "h" else finish) for o in order)
+                    order.append((hidden, up_mm, i, n) if what == "h" else (finish, down_mm, i - LAG, n))
+        order = [o for o in order if (o[0], o[2], o[3]) not in ()]
         emptied, filled, h_ready = [], [], set()
 
         def pump():
@@ -257,7 +277,7 @@ def tile_cudaternaryexpertmodule_t_kernel(
         gs = keep.tile([P, SUB], F32, name="gs")
         us = keep.tile([P, SUB], F32, name="us")
         ds_col = keep.tile([P, SUB], F32, name="ds_col")
-        warm(5)
+        warm(4)
         spread(xsc_col, [(nc.vector.tensor_copy, scale_rep[:, 0, :]), (nc.scalar.copy, scale_rep[:, 1, :])])
         widen_next(1)
         warm(2)
@@ -277,7 +297,7 @@ def tile_cudaternaryexpertmodule_t_kernel(
         quantize_x(0)
         gate_mm(0, 0)
         gate_mm(0, 1)
-        widen_next(2)
+        widen_next(1)
         up_q = quantize_weight(up_grouped, "up")
         silu(0, 0)
         gate_mm(0, 2)
@@ -289,15 +309,57 @@ def tile_cudaternaryexpertmodule_t_kernel(
             empty_x(1, h)
         widen_next(2)
 
-        for i in range(N_GROUPS + LAG):
+        for i in range(N_GROUPS):
             nxt, near, old = i + 1, i + 2, i - 1
             has_old = 0 <= old < N_GROUPS
+            pooled = (i - LAG, 3) in POOL_OUT
 
-            def block(b):
+            def hid():
                 if i < N_GROUPS:
                     empty_next()
-                if i >= LAG:
+
+            def fin(j):
+                if i >= LAG and (i - LAG, j) not in POOL_OUT:
                     empty_next()
+
+            if pooled:
+                interleave_half(old, 1)
+                interleave_half(old, 0)
+                silu(i, 2)
+                pool_mm(i - LAG, 3)
+                hid()
+                fin(0)
+                hid()
+                silu(i, 3)
+                if nxt < N_GROUPS:
+                    quantize_x(nxt)
+                    gate_mm(nxt, 0)
+                quantize_h(old, 0)
+                quantize_h(old, 1)
+                pump()
+                finish_pool(i - LAG, 3)
+                if nxt < N_GROUPS:
+                    gate_mm(nxt, 1)
+                if near < N_GROUPS:
+                    turn_x(near, 0)
+                    turn_x(near, 1)
+                fin(1)
+                hid()
+                if nxt < N_GROUPS:
+                    silu(nxt, 0)
+                    gate_mm(nxt, 2)
+                    silu(nxt, 1)
+                    gate_mm(nxt, 3)
+                if near < N_GROUPS:
+                    empty_x(near, 0)
+                    empty_x(near, 1)
+                fin(2)
+                hid()
+                continue
+
+            def block(b):
+                hid()
+                fin(b)
                 widen_next((WIDEN[i] + 3 - b) // 4)
 
             if i < N_GROUPS:
@@ -346,3 +408,20 @@ def tile_cudaternaryexpertmodule_t_kernel(
                 empty_x(near, 0)
                 empty_x(near, 1)
             block(3)
+
+        a, b = N_GROUPS - 2, N_GROUPS - 1
+        interleave_half(b, 1, pool_copy)
+        interleave_half(b, 0)
+        empty_next()
+        empty_next()
+        empty_next()
+        empty_next()
+        warm(4, ps_t, "bank_t")
+        quantize_h(b, 0)
+        pump()
+        quantize_h(b, 1)
+        pump()
+        empty_next()
+        empty_next()
+        empty_next()
+        empty_next()

@@ -19,8 +19,8 @@ P = 128
 SUB = 4
 GROUP = P * SUB
 N_GROUPS = TOKENS // GROUP
-POOL_OUT = {(i, 3) for i in range(2, 6)}
-POOL_IL = {(i, 1) for i in range(3, 7)}
+POOL_OUT = set()
+POOL_IL = set()
 LAG = 2
 WIDEN = (4, 4, 3, 0, 0, 0, 0, 0, 0, 0)
 
@@ -202,7 +202,10 @@ def tile_cudaternaryexpertmodule_t_kernel(
             if i not in hg_t:
                 hg_t[i] = work.tile([P, 512, 4], BF16, name="hg", align_bytes=64)
             c = slice(256 * h, 256 * (h + 1))
-            copy(out=hg_t[i][:, c, :], in_=h_t[i][:, :, c].rearrange("p t c -> p c t"))
+            copy(
+                out=hg_t[i][:, c, :].rearrange("p (c n) t -> p c t n", n=4),
+                in_=h_t[i][:, :, c].rearrange("p t (c n) -> p c t n", n=4),
+            )
 
         def quantize_h(i, h):
             if h == 0:
@@ -312,54 +315,12 @@ def tile_cudaternaryexpertmodule_t_kernel(
         for i in range(N_GROUPS):
             nxt, near, old = i + 1, i + 2, i - 1
             has_old = 0 <= old < N_GROUPS
-            pooled = (i - LAG, 3) in POOL_OUT
-
-            def hid():
-                if i < N_GROUPS:
-                    empty_next()
-
-            def fin(j):
-                if i >= LAG and (i - LAG, j) not in POOL_OUT:
-                    empty_next()
-
-            if pooled:
-                interleave_half(old, 1)
-                interleave_half(old, 0)
-                silu(i, 2)
-                pool_mm(i - LAG, 3)
-                hid()
-                fin(0)
-                hid()
-                silu(i, 3)
-                if nxt < N_GROUPS:
-                    quantize_x(nxt)
-                    gate_mm(nxt, 0)
-                quantize_h(old, 0)
-                quantize_h(old, 1)
-                pump()
-                finish_pool(i - LAG, 3)
-                if nxt < N_GROUPS:
-                    gate_mm(nxt, 1)
-                if near < N_GROUPS:
-                    turn_x(near, 0)
-                    turn_x(near, 1)
-                fin(1)
-                hid()
-                if nxt < N_GROUPS:
-                    silu(nxt, 0)
-                    gate_mm(nxt, 2)
-                    silu(nxt, 1)
-                    gate_mm(nxt, 3)
-                if near < N_GROUPS:
-                    empty_x(near, 0)
-                    empty_x(near, 1)
-                fin(2)
-                hid()
-                continue
 
             def block(b):
-                hid()
-                fin(b)
+                if i < N_GROUPS:
+                    empty_next()
+                if i >= LAG:
+                    empty_next()
                 widen_next((WIDEN[i] + 3 - b) // 4)
 
             if i < N_GROUPS:
@@ -369,14 +330,11 @@ def tile_cudaternaryexpertmodule_t_kernel(
             block(0)
             if nxt < N_GROUPS:
                 quantize_x(nxt)
-                gate_mm(nxt, 0)
                 pump()
             if has_old:
                 interleave_half(old, 0)
             if i < N_GROUPS:
                 silu(i, 3)
-            if nxt < N_GROUPS:
-                gate_mm(nxt, 1)
             if near < N_GROUPS:
                 turn_x(near, 0)
             if i == 0:
@@ -393,8 +351,9 @@ def tile_cudaternaryexpertmodule_t_kernel(
             if has_old:
                 quantize_h(old, 0)
             if nxt < N_GROUPS:
+                gate_mm(nxt, 0)
                 silu(nxt, 0)
-                gate_mm(nxt, 2)
+                gate_mm(nxt, 1)
                 silu(nxt, 1)
             block(2)
             if i == 0:
@@ -403,14 +362,16 @@ def tile_cudaternaryexpertmodule_t_kernel(
             if has_old:
                 quantize_h(old, 1)
             if nxt < N_GROUPS:
-                gate_mm(nxt, 3)
+                gate_mm(nxt, 2)
             if near < N_GROUPS and i > 0:
                 empty_x(near, 0)
                 empty_x(near, 1)
             block(3)
+            if nxt < N_GROUPS:
+                gate_mm(nxt, 3)
 
         a, b = N_GROUPS - 2, N_GROUPS - 1
-        interleave_half(b, 1, pool_copy)
+        interleave_half(b, 1, nc.vector.tensor_copy)
         interleave_half(b, 0)
         empty_next()
         empty_next()

from contextlib import ExitStack

import concourse.mybir as mybir
from concourse.masks import make_identity

TOKENS, H, I = 4096, 512, 512
FLOPS = 3 * 2 * TOKENS * H * I

F32 = mybir.dt.float32
BF16 = mybir.dt.bfloat16
U32 = mybir.dt.uint32
U8 = mybir.dt.uint8
FP8 = mybir.dt.float8_e4m3fn
FP8X4 = mybir.dt.float8_e4m3fn_x4
MULT = mybir.AluOpType.mult
SILU = mybir.ActivationFunctionType.Silu

P = 128
SUB = 4
GROUP = P * SUB
N_GROUPS = TOKENS // GROUP
POOL_OUT = set()
POOL_IL = set()
LAG = 2
WIDEN = (4, 4, 3, 0, 0, 0, 0, 0, 0, 0)


def tile_cudaternaryexpertmodule_t_kernel(
    tc, x_bytes, x_scale, gate_w, up_w, down_w, gate_s, up_s, down_s, out
):
    nc = tc.nc
    x_view = x_bytes.rearrange("b s k -> (b s) k").rearrange("(g p j) k -> g p j k", p=P, j=SUB)
    out_view = out.rearrange("b s k -> (b s) k").rearrange("(g p j) k -> g p j k", p=P, j=SUB)

    with ExitStack() as ctx:
        keep = ctx.enter_context(tc.tile_pool(name="keep", bufs=1))
        xin = ctx.enter_context(tc.tile_pool(name="xin", bufs=N_GROUPS))
        win = ctx.enter_context(tc.tile_pool(name="win", bufs=3))
        work = ctx.enter_context(tc.tile_pool(name="work", bufs=2))
        outp = ctx.enter_context(tc.tile_pool(name="outp", bufs=3))
        ps_t = ctx.enter_context(tc.psum_pool(name="ps_t", bufs=2))
        ps_g = ctx.enter_context(tc.psum_pool(name="ps_g", bufs=2))
        ps_m = ctx.enter_context(tc.psum_pool(name="ps_m", bufs=4))
        ctx.enter_context(tc.manual_schedule())

        zeros = keep.tile([P, 512], BF16, name="zeros")
        nc.vector.memset(zeros[:], 0.0)

        def warm(n, pool=ps_m, tag="m_ps"):
            bank = pool.tile([P, 512], F32, name=tag)
            for k in range(n):
                nc.tensor.matmul(out=bank[:], lhsT=zeros[:, 0:P], rhs=zeros[:], start=True, stop=True)

        ident = keep.tile([P, P], F32, name="ident")
        make_identity(nc, ident[:])

        xsc_col = keep.tile([P, SUB], F32, name="xsc_col")
        gs_raw = keep.tile([P, SUB], BF16, name="gs_raw")
        us_raw = keep.tile([P, SUB], BF16, name="us_raw")
        ds_raw = keep.tile([P, SUB], BF16, name="ds_raw")
        nc.scalar.dma_start(out=xsc_col[:], in_=x_scale.rearrange("a b k -> (a b k)").rearrange("(p t) -> p t", t=SUB))
        nc.scalar.dma_start(out=gs_raw[:], in_=gate_s.rearrange("(p t) -> p t", t=SUB))
        nc.scalar.dma_start(out=us_raw[:], in_=up_s.rearrange("(p t) -> p t", t=SUB))
        nc.scalar.dma_start(out=ds_raw[:], in_=down_s.rearrange("(p t) -> p t", t=SUB))
        scale_rep = keep.tile([P, 2, H], F32, name="scale_rep")
        ds_rep = keep.tile([P, H], F32, name="ds_rep")

        def spread(col, copies):
            bank = ps_g.tile([P, SUB, P], F32, name="g_ps")
            for t in range(SUB):
                nc.tensor.transpose(bank[:, t, :], col[:, t : t + 1].to_broadcast([P, P]), ident[:])
            for copy, dst in copies:
                copy(out=dst.rearrange("p (n t) -> p n t", t=SUB), in_=bank[:].rearrange("p t n -> p n t"))

        x_tiles = [xin.tile([P, SUB, H], U8, name="x8") for i in range(N_GROUPS)]
        gate_raw = win.tile([P, SUB, H], BF16, name="w_raw")
        up_raw = win.tile([P, SUB, H], BF16, name="w_raw")
        down_raw = win.tile([P, SUB, H], BF16, name="w_raw")

        def load(dst, src, parts):
            n = SUB // parts
            for h in range(parts):
                nc.sync.dma_start(out=dst[:, h * n : (h + 1) * n, :], in_=src[:, h * n : (h + 1) * n, :])

        load(x_tiles[0], x_view[0], 2)
        load(gate_raw, gate_w.rearrange("(m t) k -> m t k", t=SUB), 2)
        load(up_raw, up_w.rearrange("(m t) k -> m t k", t=SUB), 2)
        load(x_tiles[1], x_view[1], 1)
        load(down_raw, down_w.rearrange("(r p) k -> p r k", p=P), 2)
        for i in range(2, N_GROUPS):
            load(x_tiles[i], x_view[i], 1)

        def transpose_half(raw, h):
            words = raw.bitcast(F32)
            bank = ps_t.tile([P, 2, 2, P], F32, name="bank_t")
            for jj in range(2):
                for u in range(2):
                    w0 = (2 * h + jj) * (H // 2)
                    nc.tensor.transpose(bank[:, jj, u, :], words[:, w0 + u : w0 + H // 2 : 2], ident[:])
            return bank

        def empty_half(bank, h, grouped, copy=nc.scalar.copy):
            half = grouped.bitcast(F32)[:, h * 512 : (h + 1) * 512]
            copy(
                out=half.rearrange("p (j n u) -> p j n u", j=2, u=2),
                in_=bank[:].rearrange("p j u n -> p j n u"),
            )

        def quantize(codes, scales, grouped):
            nc.vector.quantize_mx(out=codes.bitcast(FP8X4), scales=scales, in_=grouped)

        def turn_weight(raw, copies=(nc.scalar.copy, nc.scalar.copy)):
            grouped = work.tile([P, SUB * H], BF16, name="w_grouped", align_bytes=64)
            flat = raw[:].rearrange("p j k -> p (j k)")
            for h in range(2):
                empty_half(transpose_half(flat, h), h, grouped[:], copies[h])
            return grouped

        def quantize_weight(grouped, name):
            codes = keep.tile([P, 512], U32, name=name + "_codes", align_bytes=64)
            scales = keep.tile([P, 512], U8, name=name + "_scales", align_bytes=64)
            quantize(codes[:], scales[:], grouped[:])
            return codes, scales

        xs_t, xg_t, xq_t, sg_t, h_t, hg_t, hq_t, o_t, x_banks = {}, {}, {}, {}, {}, {}, {}, {}, {}
        g_ps, u_ps, d_ps = {}, {}, {}

        def widen(i, j0, n=1):
            if j0 == 0:
                xs_t[i] = work.tile([P, SUB * H], BF16, name="xs", bufs=N_GROUPS, align_bytes=64)
            nc.vector.tensor_tensor(
                out=xs_t[i][:, j0 * H : (j0 + n) * H],
                in0=x_tiles[i][:, j0 : j0 + n, :].rearrange("p j k -> p (j k)").bitcast(FP8),
                in1=scale_rep[:, 0:n, :].rearrange("p r k -> p (r k)"),
                op=MULT,
            )

        todo = [(i, j) for i in range(N_GROUPS) for j in range(0, SUB, 2)]

        def widen_next(n):
            for k in range(n):
                if todo:
                    i, j = todo.pop(0)
                    widen(i, j, 2)

        def turn_x(i, h):
            x_banks[i, h] = transpose_half(xs_t[i][:], h)

        def empty_x(i, h, copy=nc.scalar.copy):
            if h == 0:
                xg_t[i] = work.tile([P, SUB * H], BF16, name="xg", bufs=3, align_bytes=64)
            empty_half(x_banks[i, h], h, xg_t[i][:], copy)

        def quantize_x(i):
            c = work.tile([P, 512], U32, name="xc", align_bytes=64)
            s = work.tile([P, 512], U8, name="xsc", align_bytes=64)
            quantize(c[:], s[:], xg_t[i][:])
            xq_t[i] = (c, s)

        def mx(dst, lhs, t, rhs):
            c = slice(P * t, P * (t + 1))
            nc.tensor.matmul_mx(
                out=dst,
                lhsT=lhs[0][:, c].bitcast(FP8X4),
                lhsT_scale=lhs[1][:, c],
                rhs=rhs[0][:].bitcast(FP8X4),
                rhs_scale=rhs[1][:],
                start=True,
                stop=True,
            )

        def gate_mm(i, t):
            g_ps[t] = ps_g.tile([P, 512], F32, name="g_ps")
            mx(g_ps[t][:], gate_q, t, xq_t[i])

        def up_mm(i, t):
            u_ps[i, t] = ps_m.tile([P, 512], F32, name="m_ps")
            mx(u_ps[i, t][:], up_q, t, xq_t[i])

        def down_mm(i, j):
            d_ps[i, j] = ps_m.tile([P, 512], F32, name="m_ps")
            mx(d_ps[i, j][:], hq_t[i], j, down_q)

        def silu(i, t):
            if t == 0:
                sg_t[i] = work.tile([P, SUB, 512], F32, name="sg")
            nc.scalar.activation(out=sg_t[i][:, t, :], in_=g_ps[t][:], func=SILU, scale=gs[:, t : t + 1])

        def hidden(i, t):
            if t == 0:
                h_t[i] = work.tile([P, SUB, 512], BF16, name="hid")
            nc.vector.scalar_tensor_tensor(
                out=h_t[i][:, t, :], in0=u_ps[i, t][:], scalar=us[:, t : t + 1], in1=sg_t[i][:, t, :], op0=MULT, op1=MULT
            )

        def pool_copy(out, in_):
            nc.gpsimd.tensor_scalar(out=out, in0=in_, scalar1=1.0, scalar2=0.0, op0=MULT, op1=mybir.AluOpType.add)

        def interleave_half(i, h, copy=nc.scalar.copy):
            if (i, h) in POOL_IL:
                copy = pool_copy
            if i not in hg_t:
                hg_t[i] = work.tile([P, 512, 4], BF16, name="hg", align_bytes=64)
            c = slice(256 * h, 256 * (h + 1))
            copy(
                out=hg_t[i][:, c, :].rearrange("p (c n) t -> p c t n", n=4),
                in_=h_t[i][:, :, c].rearrange("p t (c n) -> p c t n", n=4),
            )

        def quantize_h(i, h):
            if h == 0:
                hq_t[i] = (
                    work.tile([P, 512], U32, name="hc", align_bytes=64),
                    work.tile([P, 512], U8, name="hsc", align_bytes=64),
                )
            c = slice(256 * h, 256 * (h + 1))
            h_ready.add((i, h))
            quantize(hq_t[i][0][:, c], hq_t[i][1][:, c], hg_t[i][:, c, :].rearrange("p c t -> p (c t)"))

        done = set()

        def store(i, j):
            done.add((i, j))
            a = j - j % 2
            if i == N_GROUPS - 1:
                nc.sync.dma_start(out=out_view[i][:, j, :], in_=o_t[i][:, j, :])
            elif (i, a) in done and (i, a + 1) in done:
                nc.sync.dma_start(out=out_view[i][:, a : a + 2, :], in_=o_t[i][:, a : a + 2, :])

        def finish(i, j):
            if i not in o_t:
                o_t[i] = outp.tile([P, SUB, 512], F32, name="o", bufs=4)
            nc.vector.tensor_tensor(out=o_t[i][:, j, :], in0=d_ps[i, j][:], in1=ds_rep[:], op=MULT)
            store(i, j)

        def pool_mm(i, j):
            d_ps[i, j] = ps_g.tile([P, 512], F32, name="g_ps")
            mx(d_ps[i, j][:], hq_t[i], j, down_q)

        def finish_pool(i, j):
            if i not in o_t:
                o_t[i] = outp.tile([P, SUB, 512], F32, name="o", bufs=4)
            raw = work.tile([P, 512], F32, name="o_raw")
            nc.scalar.copy(out=raw[:], in_=d_ps[i, j][:])
            nc.gpsimd.tensor_tensor(out=o_t[i][:, j, :], in0=raw[:], in1=ds_rep[:], op=MULT)
            store(i, j)

        order = []
        for i in range(N_GROUPS + LAG):
            for t in range(SUB):
                if i >= LAG and (i - LAG, 3) in POOL_OUT:
                    continue
                if i < N_GROUPS:
                    order.append((hidden, up_mm, i, t))
                if i >= LAG:
                    order.append((finish, down_mm, i - LAG, t))
            if i >= LAG and (i - LAG, 3) in POOL_OUT:
                for what in "hfhfhfh":
                    n = sum(o[2] == (i if what == "h" else i - LAG) and o[0] == (hidden if what == "h" else finish) for o in order)
                    order.append((hidden, up_mm, i, n) if what == "h" else (finish, down_mm, i - LAG, n))
        order = [o for o in order if (o[0], o[2], o[3]) not in ()]
        emptied, filled, h_ready = [], [], set()

        def pump():
            while len(filled) < min(len(order), len(emptied) + 4):
                what, filler, i, t = order[len(filled)]
                if filler == up_mm and i not in xq_t:
                    return
                if filler == down_mm and (i, t // 2) not in h_ready:
                    return
                filler(i, t)
                filled.append(t)

        def empty_next():
            what, filler, i, t = order[len(emptied)]
            what(i, t)
            emptied.append(t)
            pump()

        gs = keep.tile([P, SUB], F32, name="gs")
        us = keep.tile([P, SUB], F32, name="us")
        ds_col = keep.tile([P, SUB], F32, name="ds_col")
        warm(4)
        spread(xsc_col, [(nc.vector.tensor_copy, scale_rep[:, 0, :]), (nc.scalar.copy, scale_rep[:, 1, :])])
        widen_next(1)
        warm(2)
        gate_grouped = turn_weight(gate_raw)
        widen_next(1)
        warm(2)
        for h in range(2):
            turn_x(0, h)
            empty_x(0, h)
        gate_q = quantize_weight(gate_grouped, "gate")
        warm(2)
        up_grouped = turn_weight(up_raw)
        nc.vector.tensor_copy(out=gs[:], in_=gs_raw[:])
        nc.vector.tensor_copy(out=us[:], in_=us_raw[:])
        nc.vector.tensor_copy(out=ds_col[:], in_=ds_raw[:])
        widen_next(1)
        quantize_x(0)
        gate_mm(0, 0)
        gate_mm(0, 1)
        widen_next(1)
        up_q = quantize_weight(up_grouped, "up")
        silu(0, 0)
        gate_mm(0, 2)
        silu(0, 1)
        gate_mm(0, 3)
        pump()
        for h in range(2):
            turn_x(1, h)
            empty_x(1, h)
        widen_next(2)

        for i in range(N_GROUPS):
            nxt, near, old = i + 1, i + 2, i - 1
            has_old = 0 <= old < N_GROUPS

            def block(b):
                if i < N_GROUPS:
                    empty_next()
                if i >= LAG:
                    empty_next()
                widen_next((WIDEN[i] + 3 - b) // 4)

            if i < N_GROUPS:
                silu(i, 2)
            if old == N_GROUPS - 1:
                interleave_half(old, 1, nc.vector.tensor_copy)
            block(0)
            if nxt < N_GROUPS:
                quantize_x(nxt)
                pump()
            if has_old:
                interleave_half(old, 0)
            if i < N_GROUPS:
                silu(i, 3)
            if near < N_GROUPS:
                turn_x(near, 0)
            if i == 0:
                empty_x(near, 0)
            block(1)
            if has_old and old < N_GROUPS - 1:
                interleave_half(old, 1)
            if near < N_GROUPS:
                turn_x(near, 1)
            if i == 0:
                empty_x(near, 1)
            if i == 1:
                down_q = quantize_weight(down_grouped, "down")
            if has_old:
                quantize_h(old, 0)
            if nxt < N_GROUPS:
                gate_mm(nxt, 0)
                silu(nxt, 0)
                gate_mm(nxt, 1)
                silu(nxt, 1)
            block(2)
            if i == 0:
                down_grouped = turn_weight(down_raw)
                spread(ds_col, [(nc.scalar.copy, ds_rep[:])])
            if has_old:
                quantize_h(old, 1)
            if nxt < N_GROUPS:
                gate_mm(nxt, 2)
            if near < N_GROUPS and i > 0:
                empty_x(near, 0)
                empty_x(near, 1)
            block(3)
            if nxt < N_GROUPS:
                gate_mm(nxt, 3)

        a, b = N_GROUPS - 2, N_GROUPS - 1
        interleave_half(b, 1, nc.vector.tensor_copy)
        interleave_half(b, 0)
        empty_next()
        empty_next()
        empty_next()
        empty_next()
        warm(4, ps_t, "bank_t")
        quantize_h(b, 0)
        pump()
        quantize_h(b, 1)
        pump()
        empty_next()
        empty_next()
        empty_next()
        empty_next()
